import numpy as np
import ml_dtypes


def mxq(x, axis, fmt="e4m3"):
    dtype, down = {"e4m3": (ml_dtypes.float8_e4m3fn, 7), "e5m2": (ml_dtypes.float8_e5m2, 14)}[fmt]
    v = np.moveaxis(np.asarray(x, np.float32).astype(ml_dtypes.bfloat16).astype(np.float64), axis, -1)
    blocks = v.reshape(v.shape[:-1] + (-1, 32))
    amax = np.abs(blocks).max(-1, keepdims=True)
    byte = np.maximum(np.where(amax > 0, np.frexp(amax)[1] - 1 + 127, 0) - down, 1)
    scale = np.exp2(byte - 127.0)
    codes = (blocks / scale).astype(np.float32).astype(dtype).astype(np.float64)
    return np.moveaxis((codes * scale).reshape(v.shape), -1, axis)


WIDE = False


def mx_kscale(k):
    if not WIDE:
        return np.ones(k)
    levels = np.array([10, -10, 5, -5, 0])
    if k % 512:
        return np.exp2(np.random.permutation(np.resize(levels, k // 32))).repeat(32)
    a = np.empty((k // 512, 16))
    for p in range(k // 512):
        a[p, :8] = np.random.permutation(np.resize(levels, 8))
        for g in range(8):
            far = levels[np.abs(levels - a[p, g]) >= 10]
            a[p, g + 8] = far[np.random.randint(len(far))]
    return np.exp2(a.ravel()).repeat(32)


BF16 = ml_dtypes.bfloat16


def bf(x):
    return np.asarray(x, np.float32).astype(BF16)


def f64(x):
    return np.asarray(x).astype(np.float64)


E2M1 = np.array([0.0, 0.5, 1.0, 1.5, 2.0, 3.0, 4.0, 6.0, -0.0, -0.5, -1.0, -1.5, -2.0, -3.0, -4.0, -6.0])


def pack_weight(w, fmt):
    k, n = w.shape
    w = f64(bf(w)).reshape(k // 32, 32, n)
    amax = np.abs(w).max(1)
    if fmt == "e4m3":
        byte = np.frexp(amax)[1] - 1 + 127 - 7
    else:
        mant, ex = np.frexp(amax / 6.0)
        byte = np.where(mant > 0.5, ex, ex - 1) + 127
    byte = np.clip(np.where(amax > 0, byte, 1), 1, 254)
    scaled = (w * np.exp2(127.0 - byte)[:, None, :]).reshape(k, n).astype(np.float32)
    by_word = np.ascontiguousarray(scaled.reshape(k // 512, 128, 4, n).transpose(0, 1, 3, 2))
    if fmt == "e4m3":
        words = by_word.astype(ml_dtypes.float8_e4m3fn).view(np.uint8)
    else:
        c = by_word.astype(ml_dtypes.float4_e2m1fn).view(np.uint8) & 0xF
        words = c[..., 0::2] | (c[..., 1::2] << 4)
    return np.ascontiguousarray(words), np.ascontiguousarray(byte.astype(np.uint8).reshape(k // 512, 16, n))


def unpack_weight(words, scales, fmt):
    g, p, n, _ = words.shape
    if fmt == "e4m3":
        vals = np.ascontiguousarray(words).view(ml_dtypes.float8_e4m3fn).astype(np.float64)
    else:
        nib = np.empty((g, p, n, 4), np.uint8)
        nib[..., 0::2] = words & 0xF
        nib[..., 1::2] = words >> 4
        vals = E2M1[nib]
    vals = vals * np.repeat(np.exp2(scales.astype(np.float64) - 127.0), 8, axis=1)[..., None]
    return vals.transpose(0, 1, 3, 2).reshape(g * 512, n)
def pack4(w):
    words, scales = pack_weight(w, "e2m1")
    return words.reshape(words.shape[0], 128, -1), scales


def unpack4(words, scales):
    return unpack_weight(words.reshape(words.shape[0], 128, -1, 2), scales, "e2m1")


B, L, N, RS, D, H, A, F = 4, 4, 128, 16, 512, 8, 64, 2048
S = L * (N + RS)
EPS = 1e-05


def rmsnorm(x, w):
    return x / np.sqrt(np.mean(x * x, -1, keepdims=True) + EPS) * w


def silu(v):
    return v / (1.0 + np.exp(-v))


def draw0():
    s, t = mx_kscale(D), mx_kscale(D)
    o_attn = bf(np.random.standard_normal((B, S, D)) * 0.14 * s)
    xm = bf(np.random.standard_normal((B, S, D)))
    attn_o_w_words, attn_o_w_scales = pack4(np.random.standard_normal((D, D)) * 3.0 / np.sqrt(D) / s[:, None])
    ffn_norm_w = bf((1.0 + 0.1 * np.random.standard_normal(D)) * t)
    ffn_up_w_words, ffn_up_w_scales = pack4(np.random.standard_normal((D, 2 * F)) / np.sqrt(D) / t[:, None])
    return {'o_attn': o_attn,
            'xm': xm,
            'attn_o_w_words': attn_o_w_words,
            'attn_o_w_scales': attn_o_w_scales,
            'ffn_norm_w': ffn_norm_w,
            'ffn_up_w_words': ffn_up_w_words,
            'ffn_up_w_scales': ffn_up_w_scales}


def core(o_attn, xm, attn_o_w_words, attn_o_w_scales, ffn_norm_w, ffn_up_w_words, ffn_up_w_scales):
    x2 = (mxq(f64(o_attn), 2, 'e4m3') @ unpack4(attn_o_w_words, attn_o_w_scales)) + f64(xm)
    xn2 = rmsnorm(x2, f64(ffn_norm_w))
    u1, u2 = np.split(mxq(xn2, 2, 'e4m3') @ unpack4(ffn_up_w_words, ffn_up_w_scales), 2, axis=-1)
    return x2, silu(u1) * u2


def e4m3fn_bytes(y):
    return np.clip(np.asarray(y, np.float64), -448.0, 448.0).astype(np.float32).astype(ml_dtypes.float8_e4m3fn).view(np.uint8)


def e4m3fn_values(b):
    return np.asarray(b, np.uint8).view(ml_dtypes.float8_e4m3fn).astype(np.float64)


def setup_inputs():
    d = draw0()
    x0 = np.asarray(d['o_attn']).astype(np.float64)
    s = (np.max(np.abs(x0), axis=(0, 1), keepdims=True) / 448.0).astype(np.float32)
    out = {}
    for k, v in d.items():
        if k == 'o_attn':
            out['o_attn_bytes'] = e4m3fn_bytes(x0 / s.astype(np.float64))
            out['o_attn_scale'] = s
        else:
            out[k] = v
    return out


def reference(o_attn_bytes, o_attn_scale, xm, attn_o_w_words, attn_o_w_scales, ffn_norm_w, ffn_up_w_words, ffn_up_w_scales):
    return core(e4m3fn_values(o_attn_bytes) * o_attn_scale.astype(np.float64), xm, attn_o_w_words, attn_o_w_scales, ffn_norm_w, ffn_up_w_words, ffn_up_w_scales)

from contextlib import ExitStack

import concourse.mybir as mybir
from concourse.masks import make_identity

F32 = mybir.dt.float32
BF16 = mybir.dt.bfloat16
U32 = mybir.dt.uint32
U8 = mybir.dt.uint8
I32 = mybir.dt.int32
FP8 = mybir.dt.float8_e4m3fn
FP8X4 = mybir.dt.float8_e4m3fn_x4
FP4X4 = mybir.dt.float4_e2m1fn_x4
ALU = mybir.AluOpType
ACT = mybir.ActivationFunctionType

P = 128
TOKENS = 4 * 576
NT = TOKENS // P
D = 512
F = 2048
FC = 512
NC = F // FC
EPS = 1e-5

FLOPS = 2 * TOKENS * D * (D + 2 * F)

GROUPS = [(0, 1), (1, 1)] + [(t, 2) for t in range(2, NT, 2)]
LOADS = [(0, 1), (1, 1), (2, 4), (6, 6), (12, 6)]


def tile_model_pb_w4_kernel(
    tc, o_bytes, o_scale, xm, wo_words, wo_scales, gain, wu_words, wu_scales, out_x2, out_h
):
    nc = tc.nc
    o_hbm = o_bytes.rearrange("b s d -> (b s) d").rearrange("(p n) d -> p n d", n=NT)
    xm_hbm = xm.rearrange("b s d -> (b s) d").rearrange("(p n) d -> p n d", n=NT)
    x2_hbm = out_x2.rearrange("b s d -> (b s) d").rearrange("(p n) d -> p n d", n=NT)
    h_hbm = out_h.rearrange("b s f -> (b s) f").rearrange("(p n) f -> p n f", n=NT)

    with ExitStack() as ctx:
        keep = ctx.enter_context(tc.tile_pool(name="keep", bufs=1))
        work = ctx.enter_context(tc.tile_pool(name="work", bufs=2))
        psum = ctx.enter_context(tc.psum_pool(name="psum", bufs=1))
        ctx.enter_context(tc.manual_schedule())

        wo = keep.tile([P, 2 * D], U8, name="wo", align_bytes=64)
        wo_sc = keep.tile([P, D], U8, name="wo_sc", align_bytes=64)
        wu = []
        for half in range(2):
            w_half = keep.tile([P, 2, 2 * F // 2], U8, name="wu%d" % half, align_bytes=64)
            wu.append(w_half)
        wu_sc = keep.tile([P, 2 * F], U8, name="wu_sc", align_bytes=64)
        osc = keep.tile([P, 4], F32, name="osc")
        gain_row = keep.tile([P, D], BF16, name="gain_row")
        gain_sb = keep.tile([P, D], F32, name="gain_sb")
        ones = keep.tile([P, P], BF16, name="ones")
        ident = keep.tile([P, P], F32, name="ident")
        neg_half = keep.tile([P, 1], F32, name="neg_half")
        warm = keep.tile([P, 1], F32, name="warm")
        warm_out = keep.tile([P, 1], F32, name="warm_out")
        ob_in = []
        xm_in = []
        for i, (t0, n) in enumerate(LOADS):
            bt = keep.tile([P, n, D], U8, name="codes_in%d" % i)
            xt = keep.tile([P, n, D], BF16, name="xm_in%d" % i)
            ob_in.append(bt)
            xm_in.append(xt)

        def locate(t):
            for i, (t0, n) in enumerate(LOADS):
                if t < t0 + n:
                    return i, t - t0

        nc.vector.memset(warm[:], 0.0)
        nc.scalar.activation(out=warm_out[:], in_=warm[:], func=ACT.Silu)
        nc.vector.memset(wo_sc[:].bitcast(I32), 0)
        nc.vector.memset(gain_row[:], 0.0)
        nc.vector.memset(wu_sc[:].bitcast(I32), 0)
        make_identity(nc, ident[:])
        nc.gpsimd.memset(ones[:], 1.0)
        nc.gpsimd.memset(neg_half[:], -0.5)

        def load_codes(i):
            t0, n = LOADS[i]
            nc.sync.dma_start(out=ob_in[i][:], in_=o_hbm[:, t0 : t0 + n, :])

        def load_xm(i):
            t0, n = LOADS[i]
            nc.sync.dma_start(out=xm_in[i][:], in_=xm_hbm[:, t0 : t0 + n, :])

        load_codes(0)
        nc.sync.dma_start(out=osc[:], in_=o_scale.rearrange("a b (p t) -> p (a b t)", t=4))
        nc.sync.dma_start(out=wo[:].bitcast(I32), in_=wo_words.rearrange("g p n -> (g p) n").bitcast(I32))
        for q in range(4):
            nc.sync.dma_start(
                out=wo_sc[32 * q : 32 * q + 4, :].bitcast(I32),
                in_=wo_scales.rearrange("g r n -> (g r) n")[4 * q : 4 * q + 4, :].bitcast(I32),
            )
        nc.scalar.dma_start(out=gain_row[0:1, :], in_=gain.unsqueeze(0))
        load_xm(0)
        load_codes(1)
        load_xm(1)
        load_codes(2)
        for q in range(4):
            nc.sync.dma_start(
                out=wu_sc[32 * q : 32 * q + 4, :].bitcast(I32),
                in_=wu_scales.rearrange("g r n -> (g r) n")[4 * q : 4 * q + 4, :].bitcast(I32),
            )
        wu_hbm = wu_words.rearrange("g p n -> (g p) n").rearrange("p (s n) -> p s n", s=2)
        for half in range(2):
            nc.sync.dma_start(
                out=wu[half][:].bitcast(I32), in_=wu_hbm[:, :, half * F : (half + 1) * F].bitcast(I32)
            )
        load_xm(2)
        load_codes(3)
        load_xm(3)
        load_codes(4)
        load_xm(4)

        state = {}

        def valid(g):
            return 0 <= g < len(GROUPS)

        def widen(g):
            if not valid(g):
                return
            t0, n = GROUPS[g]
            i, j = locate(t0)
            ob = work.tile([P, 2 * D], BF16, name="ob", bufs=3)
            nc.scalar.copy(
                out=ob[:, : n * D], in_=ob_in[i][:, j : j + n, :].rearrange("p n d -> p (n d)").bitcast(FP8)
            )
            state["ob", g] = ob

        def turn_o(g):
            if not valid(g):
                return
            t0, n = GROUPS[g]
            ob = state["ob", g]
            to = psum.tile([P, 2, 2 * P], F32, name="to", bufs=1)
            words = ob[:].bitcast(F32)
            for i in range(n):
                for u in range(2):
                    nc.tensor.transpose(
                        to[:, u, P * i : P * (i + 1)], words[:, 256 * i + u : 256 * (i + 1) : 2], ident[:]
                    )
            state["to", g] = to

        def scale_o(g):
            if not valid(g):
                return
            t0, n = GROUPS[g]
            to = state["to", g]
            go = work.tile([P, 2 * P, 4], BF16, name="go", bufs=2, align_bytes=64)
            view = to[:].rearrange("p u r -> p (u r)").bitcast(BF16).rearrange("p (u r e) -> p r u e", u=2, e=2)
            nc.vector.tensor_tensor(
                out=go[:, : n * P, :].rearrange("p r (u e) -> p r u e", u=2),
                in0=view[:, : n * P, :, :],
                in1=osc[:].rearrange("p (u e) -> p u e", u=2).unsqueeze(1).to_broadcast([P, n * P, 2, 2]),
                op=ALU.mult,
            )
            state["go", g] = go

        def quant_o(g):
            if not valid(g):
                return
            t0, n = GROUPS[g]
            go = state["go", g]
            oc = work.tile([P, 2 * P], U32, name="oc", bufs=4, align_bytes=64)
            o_sc = work.tile([P, 2 * P], U8, name="osc_q", bufs=4, align_bytes=64)
            nc.vector.quantize_mx(
                out=oc[:, : n * P].bitcast(FP8X4),
                scales=o_sc[:, : n * P],
                in_=go[:, : n * P, :].rearrange("p r t -> p (r t)"),
            )
            state["oc", g] = (oc, o_sc)

        def mm1(g, i):
            if not valid(g) or i >= GROUPS[g][1]:
                return
            oc, o_sc = state["oc", g]
            m1 = psum.tile([P, D], F32, name="m1", bufs=1)
            nc.tensor.matmul_mx(
                out=m1[:],
                lhsT=oc[:, P * i : P * (i + 1)].bitcast(FP8X4),
                lhsT_scale=o_sc[:, P * i : P * (i + 1)],
                rhs=wo[:].bitcast(FP4X4),
                rhs_scale=wo_sc[:],
                start=True,
                stop=True,
            )
            state["m1", g, i] = m1

        def resid(g, i):
            if not valid(g) or i >= GROUPS[g][1]:
                return
            t0, n = GROUPS[g]
            if i == 0:
                x2 = work.tile([P, 2, D], F32, name="x2", bufs=3)
                state["x2", g] = x2
            x2 = state["x2", g]
            li, lj = locate(t0 + i)
            nc.vector.tensor_tensor(
                out=x2[:, i, :], in0=state["m1", g, i][:], in1=xm_in[li][:, lj, :], op=ALU.add
            )
            if i == n - 1:
                nc.sync.dma_start(out=x2_hbm[:, t0 : t0 + n, :], in_=x2[:, :n, :])

        def gain_mul(g, i):
            if not valid(g) or i >= GROUPS[g][1]:
                return
            xw = work.tile([P, D], F32, name="xw", bufs=3)
            nc.gpsimd.tensor_tensor(out=xw[:], in0=state["x2", g][:, i, :], in1=gain_sb[:], op=ALU.mult)
            state["xw", g, i] = xw

        def square(g, i):
            if not valid(g) or i >= GROUPS[g][1]:
                return
            junk = work.tile([P, D], BF16, name="junk", bufs=2)
            ss = work.tile([P, 1], F32, name="ss", bufs=4)
            nc.scalar.activation(out=junk[:], in_=state["x2", g][:, i, :], func=ACT.Square, accum_out=ss[:])
            state["ss", g, i] = ss

        def norm(g, i):
            if not valid(g) or i >= GROUPS[g][1]:
                return
            ss = state["ss", g, i]
            var = work.tile([P, 1], F32, name="var", bufs=4)
            rstd = work.tile([P, 1], F32, name="rstd", bufs=4)
            nc.gpsimd.tensor_scalar(
                out=var[:], in0=ss[:], scalar1=1.0 / D, scalar2=EPS, op0=ALU.mult, op1=ALU.add
            )
            nc.gpsimd.tensor_tensor(out=rstd[:], in0=var[:], in1=neg_half[:], op=ALU.pow)
            if i == 0:
                xn = work.tile([P, 2, 2, P, 2], BF16, name="xn", bufs=3)
                state["xn", g] = xn
            xn = state["xn", g]
            nc.gpsimd.tensor_scalar(
                out=xn[:, i],
                in0=state["xw", g, i][:].rearrange("p (w u e) -> p u w e", u=2, e=2),
                scalar1=rstd[:],
                scalar2=1.0,
                op0=ALU.mult,
                op1=ALU.mult,
            )

        def turn_x(g):
            if not valid(g):
                return
            t0, n = GROUPS[g]
            xn = state["xn", g]
            tx = psum.tile([P, 2, 2 * P], F32, name="tx", bufs=1)
            words = xn[:].rearrange("p i u w e -> p (i u w e)").bitcast(F32)
            for i in range(n):
                for u in range(2):
                    c0 = 256 * i + 128 * u
                    nc.tensor.transpose(tx[:, u, P * i : P * (i + 1)], words[:, c0 : c0 + P], ident[:])
            state["tx", g] = tx

        def copy_x(g):
            if not valid(g):
                return
            t0, n = GROUPS[g]
            tx = state["tx", g]
            gx = work.tile([P, 2 * P, 4], BF16, name="gx", bufs=2, align_bytes=64)
            words = gx[:].rearrange("p r t -> p (r t)").bitcast(F32).rearrange("p (r u) -> p r u", u=2)
            nc.scalar.copy(out=words[:, : n * P, :], in_=tx[:, :, : n * P].rearrange("p u r -> p r u"))
            state["gx", g] = gx

        def quant_x(g):
            if not valid(g):
                return
            t0, n = GROUPS[g]
            gx = state["gx", g]
            xc = work.tile([P, 2 * P], U32, name="xc", bufs=2, align_bytes=64)
            xs = work.tile([P, 2 * P], U8, name="xs", bufs=2, align_bytes=64)
            nc.vector.quantize_mx(
                out=xc[:, : n * P].bitcast(FP8X4),
                scales=xs[:, : n * P],
                in_=gx[:, : n * P, :].rearrange("p r t -> p (r t)"),
            )
            state["xc", g] = (xc, xs)

        def step(g, k):
            t0, n = GROUPS[g]
            i, c = k // NC, k % NC
            t = t0 + i
            xc, xs = state["xc", g]
            u1 = psum.tile([P, FC], F32, name="u1", bufs=2)
            u2 = psum.tile([P, FC], F32, name="u2", bufs=3)
            for s, u in ((0, u1), (1, u2)):
                cols = slice(FC * 2 * (c % 2), FC * 2 * (c % 2 + 1))
                nc.tensor.matmul_mx(
                    out=u[:],
                    lhsT=xc[:, P * i : P * (i + 1)].bitcast(FP8X4),
                    lhsT_scale=xs[:, P * i : P * (i + 1)],
                    rhs=wu[c // 2][:, s, cols].bitcast(FP4X4),
                    rhs_scale=wu_sc[:, F * s + FC * c : F * s + FC * (c + 1)],
                    start=True,
                    stop=True,
                )
            act = work.tile([P, FC], F32, name="act", bufs=3)
            nc.scalar.activation(out=act[:], in_=u1[:], func=ACT.Silu)
            if c % 2 == 0:
                h_new = work.tile([P, 2, FC], F32, name="h", bufs=6)
                state["h"] = h_new
            h = state["h"]
            nc.vector.tensor_tensor(out=h[:, c % 2, :], in0=u2[:], in1=act[:], op=ALU.mult)
            if t == NT - 1:
                nc.sync.dma_start(out=h_hbm[:, t, FC * c : FC * (c + 1)], in_=h[:, c % 2, :])
            elif c % 2 == 1:
                nc.sync.dma_start(
                    out=h_hbm[:, t, FC * (c - 1) : FC * (c + 1)], in_=h[:].rearrange("p a b -> p (a b)")
                )

        def spread_gain():
            g_ps = psum.tile([P, FC], F32, name="u1", bufs=2)
            nc.tensor.matmul(g_ps[:], ones[:], gain_row[:], start=True, stop=True)
            nc.scalar.copy(out=gain_sb[:], in_=g_ps[:])

        ahead = {"x": 1, "m": 2, "o": 4, "w": 5}
        tasks = {
            "turn_x": (turn_x, "x", ()),
            "turn_o": (turn_o, "o", ()),
            "copy_x": (copy_x, "x", ()),
            "scale_o": (scale_o, "o", ()),
            "mm1_0": (mm1, "m", (0,)),
            "resid_0": (resid, "m", (0,)),
            "gmul_0": (gain_mul, "m", (0,)),
            "sq_0": (square, "m", (0,)),
            "nrm_0": (norm, "m", (0,)),
            "mm1_1": (mm1, "m", (1,)),
            "resid_1": (resid, "m", (1,)),
            "gmul_1": (gain_mul, "m", (1,)),
            "sq_1": (square, "m", (1,)),
            "nrm_1": (norm, "m", (1,)),
            "quant_x": (quant_x, "x", ()),
            "quant_o": (quant_o, "o", ()),
            "widen": (widen, "w", ()),
        }
        prologue = "widen:0 turn_o:0 scale_o:0 widen:1 spread:0 turn_o:1 quant_o:0 mm1_0:0 scale_o:1 widen:2 turn_o:2 widen:3 resid_0:0 quant_o:1 gmul_0:0 scale_o:2 sq_0:0 mm1_0:1 turn_o:3 nrm_0:0 resid_0:1 quant_o:2 turn_x:0 gmul_0:1 sq_0:1 scale_o:3 copy_x:0 quant_x:0 nrm_0:1 quant_o:3 widen:4"
        for entry in prologue.split(" "):
            name, g = entry.split(":")
            if name == "spread":
                spread_gain()
            else:
                fn, stage, extra = tasks[name]
                fn(int(g), *extra)
        place = {"mm1_0": -1, "resid_0": -0.7, "gmul_0": 4, "turn_x": 5, "turn_o": 3, "sq_0": 3.6, "nrm_0": 5.6, "mm1_1": -1, "copy_x": 5.3, "resid_1": 1.6, "gmul_1": 6, "scale_o": 3.3, "sq_1": 7.3, "nrm_1": 7.3, "quant_x": 5.6, "widen": 6.3, "quant_o": 5.6}
        for g in range(len(GROUPS)):
            n = GROUPS[g][1]
            for k in range(-1, n * NC):
                if k >= 0:
                    step(g, k)
                todo = []
                for r, name in enumerate(tasks):
                    where = place[name] if n == 2 else place[name] / 2
                    if (k < 0 and where < 0) or (k >= 0 and k <= where < k + 1) or (k == n * NC - 1 and where >= n * NC):
                        todo.append((where, r, name))
                for where, r, name in sorted(todo):
                    fn, stage, extra = tasks[name]
                    fn(g + ahead[stage], *extra)
